import numpy as np
import ml_dtypes


def mxq(x, axis, fmt="e4m3"):
    dtype, down = {"e4m3": (ml_dtypes.float8_e4m3fn, 7), "e5m2": (ml_dtypes.float8_e5m2, 14)}[fmt]
    v = np.moveaxis(np.asarray(x, np.float32).astype(ml_dtypes.bfloat16).astype(np.float64), axis, -1)
    blocks = v.reshape(v.shape[:-1] + (-1, 32))
    amax = np.abs(blocks).max(-1, keepdims=True)
    byte = np.maximum(np.where(amax > 0, np.frexp(amax)[1] - 1 + 127, 0) - down, 1)
    scale = np.exp2(byte - 127.0)
    codes = (blocks / scale).astype(np.float32).astype(dtype).astype(np.float64)
    return np.moveaxis((codes * scale).reshape(v.shape), -1, axis)


WIDE = False


def mx_kscale(k):
    if not WIDE:
        return np.ones(k)
    levels = np.array([10, -10, 5, -5, 0])
    a = np.random.permutation(np.resize(levels, k // 512 * 4)).reshape(k // 512, 4)
    idx = np.arange(k)
    return np.exp2(a[idx // 512, idx % 128 // 32])


BF16 = ml_dtypes.bfloat16


def bf(x):
    return np.asarray(x, np.float32).astype(BF16)


def f64(x):
    return np.asarray(x).astype(np.float64)


E2M1 = np.array([0.0, 0.5, 1.0, 1.5, 2.0, 3.0, 4.0, 6.0, -0.0, -0.5, -1.0, -1.5, -2.0, -3.0, -4.0, -6.0])


def pack_weight(w, fmt):
    k, n = w.shape
    w = f64(bf(w)).reshape(k // 32, 32, n)
    amax = np.abs(w).max(1)
    if fmt == "e4m3":
        byte = np.frexp(amax)[1] - 1 + 127 - 7
    else:
        mant, ex = np.frexp(amax / 6.0)
        byte = np.where(mant > 0.5, ex, ex - 1) + 127
    byte = np.clip(np.where(amax > 0, byte, 1), 1, 254)
    scaled = (w * np.exp2(127.0 - byte)[:, None, :]).reshape(k, n).astype(np.float32)
    by_word = np.ascontiguousarray(scaled.reshape(k // 512, 128, 4, n).transpose(0, 1, 3, 2))
    if fmt == "e4m3":
        words = by_word.astype(ml_dtypes.float8_e4m3fn).view(np.uint8)
    else:
        c = by_word.astype(ml_dtypes.float4_e2m1fn).view(np.uint8) & 0xF
        words = c[..., 0::2] | (c[..., 1::2] << 4)
    return np.ascontiguousarray(words), np.ascontiguousarray(byte.astype(np.uint8).reshape(k // 512, 16, n))


def unpack_weight(words, scales, fmt):
    g, p, n, _ = words.shape
    if fmt == "e4m3":
        vals = np.ascontiguousarray(words).view(ml_dtypes.float8_e4m3fn).astype(np.float64)
    else:
        nib = np.empty((g, p, n, 4), np.uint8)
        nib[..., 0::2] = words & 0xF
        nib[..., 1::2] = words >> 4
        vals = E2M1[nib]
    vals = vals * np.repeat(np.exp2(scales.astype(np.float64) - 127.0), 8, axis=1)[..., None]
    return vals.transpose(0, 1, 3, 2).reshape(g * 512, n)

def pack4(w):
    words, scales = pack_weight(w, "e2m1")
    return words.reshape(words.shape[0], 128, -1), scales


def unpack4(words, scales):
    return unpack_weight(words.reshape(words.shape[0], 128, -1, 2), scales, "e2m1")


S, B, SC = 1024, 1024, 4096


def setup_inputs():
    s = mx_kscale(B)
    proba = bf((np.random.standard_normal((S, B)) * s).reshape(-1))
    cur_inven = bf(np.random.random_sample((S, SC)))
    words, scales = pack4(np.random.random_sample((B, SC)) * (16.0 / np.sqrt(B)) / s[:, None])
    avail_bundle = bf(np.random.random_sample(B) * s)
    alloc_bundle = bf(np.random.random_sample(B) * s)
    return {"proba": proba,
            "cur_inven": cur_inven,
            "bun_sc_words": words,
            "bun_sc_scales": scales,
            "avail_bundle": avail_bundle,
            "alloc_bundle": alloc_bundle}


def reference(proba, cur_inven, bun_sc_words, bun_sc_scales, avail_bundle, alloc_bundle):
    p = f64(proba).reshape(S, B)
    av = f64(avail_bundle)
    al = f64(alloc_bundle)
    over_avail = (av[None, :] - p < 0.0) & (p > 0.0)
    over_alloc = (al[None, :] + p < 0.0) & (p < 0.0)
    cm = np.where(over_avail | over_alloc, 0.01, 1.0)
    next_inven = f64(cur_inven) + (mxq(p * cm, 1, "e4m3") @ unpack4(bun_sc_words, bun_sc_scales))
    return next_inven.reshape(1, -1)

@@ -1,0 +1,204 @@
+from contextlib import ExitStack
+
+import concourse.mybir as mybir
+from concourse.masks import make_identity
+
+BF16 = mybir.dt.bfloat16
+F32 = mybir.dt.float32
+I32 = mybir.dt.int32
+U8 = mybir.dt.uint8
+U32 = mybir.dt.uint32
+FP8X4 = mybir.dt.float8_e4m3fn_x4
+FP4X4 = mybir.dt.float4_e2m1fn_x4
+ALU = mybir.AluOpType
+
+P = 128
+S, B, SC = 1024, 1024, 4096
+NT = S // P
+G = B // 512
+NB = SC // 512
+
+FLOPS = 2 * S * B * SC
+
+P_UNITS = ((0,), (1,), (2, 3), (4, 5, 6, 7))
+CUR_UNITS = ((0,), (1,), (2, 3), (4, 5), (6, 7))
+VECTOR_BANKS = (0, 1, 4, 5)
+BANK_ORDER = (0, 2, 1, 3, 4, 6, 5, 7)
+
+
+def tile_optblockv2_kernel(
+    tc, proba, cur_inven, bun_sc_words, bun_sc_scales, avail_bundle, alloc_bundle, out
+):
+    nc = tc.nc
+    p_v = proba.rearrange("(p a k) -> p a k", p=P, a=NT, k=B)
+    cur_v = cur_inven.rearrange("(p a) n -> p a n", a=NT)
+    out_v = out.rearrange("o (p a n) -> (o p) a n", p=P, a=NT, n=SC)
+    words_v = bun_sc_words.bitcast(I32).rearrange("g p w -> p g w")
+    scales_v = bun_sc_scales.bitcast(I32).rearrange("g (q r) w -> r q g w", r=4)
+
+    with ExitStack() as ctx:
+        keep = ctx.enter_context(tc.tile_pool(name="keep", bufs=1))
+        work = ctx.enter_context(tc.tile_pool(name="work", bufs=2))
+        stage = ctx.enter_context(tc.tile_pool(name="stage", bufs=5))
+        tpool = ctx.enter_context(tc.psum_pool(name="tpool", bufs=2))
+        apool = ctx.enter_context(tc.psum_pool(name="apool", bufs=6))
+
+        wsc = keep.tile([P, G, SC], U8, name="wsc", align_bytes=64)
+        nc.vector.memset(wsc[:].bitcast(I32), 0)
+        ident = keep.tile([P, P], BF16, name="ident")
+        make_identity(nc, ident[:])
+
+        av_raw = keep.tile([P, G, 4], BF16, name="av_raw")
+        al_raw = keep.tile([P, G, 4], BF16, name="al_raw")
+        p_tiles = {}
+        cur_tiles = {}
+
+        def load_p(unit):
+            t = keep.tile([P, len(unit), B], BF16, name="p%d" % unit[0])
+            nc.sync.dma_start(out=t[:], in_=p_v[:, unit[0] : unit[-1] + 1, :])
+            for i, a in enumerate(unit):
+                p_tiles[a] = t[:, i, :]
+
+        def load_cur(unit):
+            t = keep.tile([P, len(unit), SC], BF16, name="cur%d" % unit[0])
+            nc.sync.dma_start(out=t[:], in_=cur_v[:, unit[0] : unit[-1] + 1, :])
+            for i, a in enumerate(unit):
+                cur_tiles[a] = t[:, i, :]
+
+        load_p(P_UNITS[0])
+        nc.scalar.dma_start(
+            out=av_raw[:], in_=avail_bundle.rearrange("(g p t) -> p g t", g=G, p=P, t=4)
+        )
+        nc.scalar.dma_start(
+            out=al_raw[:], in_=alloc_bundle.rearrange("(g p t) -> p g t", g=G, p=P, t=4)
+        )
+        wsc_i = wsc[:].bitcast(I32)
+        for r in range(4):
+            nc.sync.dma_start(out=wsc_i[r:P:32, :, :], in_=scales_v[r])
+        w_tiles = []
+        for c in range(2):
+            w = keep.tile([P, G, SC], U8, name="w%d" % c, align_bytes=64)
+            nc.sync.dma_start(
+                out=w[:].bitcast(I32), in_=words_v[:, :, 1024 * c : 1024 * (c + 1)]
+            )
+            w_tiles.append(w)
+        load_cur(CUR_UNITS[0])
+        load_p(P_UNITS[1])
+        load_cur(CUR_UNITS[1])
+        load_p(P_UNITS[2])
+        load_cur(CUR_UNITS[2])
+        load_p(P_UNITS[3])
+        load_cur(CUR_UNITS[3])
+        load_cur(CUR_UNITS[4])
+
+        hi = keep.tile([P, G * 4], F32, name="hi")
+        lo = keep.tile([P, G * 4], F32, name="lo")
+        nc.vector.tensor_scalar(
+            out=hi[:], in0=av_raw[:].rearrange("p g t -> p (g t)"),
+            scalar1=0.0, scalar2=None, op0=ALU.max,
+        )
+        nc.vector.tensor_scalar(
+            out=lo[:], in0=al_raw[:].rearrange("p g t -> p (g t)"),
+            scalar1=-1.0, scalar2=0.0, op0=ALU.mult, op1=ALU.min,
+        )
+
+        codes = keep.tile([P, NT, G, P], U32, name="codes", align_bytes=64)
+        hsc = keep.tile([P, NT, G, P], U8, name="hsc", align_bytes=64)
+
+        tps = {}
+
+        def transposes(a):
+            tp = tpool.tile([P, G * 4, P], BF16, name="tp")
+            for g in range(G):
+                for t in range(4):
+                    nc.tensor.transpose(
+                        tp[:, 4 * g + t, :],
+                        p_tiles[a][:, 512 * g + t : 512 * (g + 1) : 4],
+                        ident[:],
+                    )
+            tps[a] = tp
+
+        def prep_steps(a):
+            tp = tps[a]
+            r = work.tile([P, G * 4, P], BF16, name="r")
+            m = work.tile([P, G * 4, P], BF16, name="m")
+            hg = work.tile([P, G, P, 4], BF16, name="hg", align_bytes=64)
+
+            def clamp(q0, q1):
+                for q in range(q0, q1):
+                    nc.vector.tensor_scalar(
+                        out=r[:, q, :], in0=tp[:, q, :],
+                        scalar1=lo[:, q : q + 1], scalar2=hi[:, q : q + 1],
+                        op0=ALU.max, op1=ALU.min,
+                    )
+
+            def inside():
+                nc.vector.tensor_tensor(out=m[:], in0=r[:], in1=tp[:], op=ALU.is_equal)
+
+            def damp(g):
+                nc.vector.scalar_tensor_tensor(
+                    out=hg[:, g, :, :],
+                    in0=m[:, 4 * g : 4 * g + 4, :].rearrange("p t s -> p s t"),
+                    scalar=0.01,
+                    in1=tp[:, 4 * g : 4 * g + 4, :].rearrange("p t s -> p s t"),
+                    op0=ALU.max, op1=ALU.mult,
+                )
+
+            def quantise():
+                nc.vector.quantize_mx(
+                    out=codes[:, a, :, :].rearrange("p g s -> p (g s)").bitcast(FP8X4),
+                    scales=hsc[:, a, :, :].rearrange("p g s -> p (g s)"),
+                    in_=hg[:].rearrange("p g s t -> p (g s t)"),
+                )
+
+            return [
+                lambda: clamp(0, 8),
+                inside,
+                lambda: (damp(0), damp(1)),
+                quantise,
+            ]
+
+        def product(a, j):
+            acc = apool.tile([P, 512], F32, name="acc")
+            w = w_tiles[j // 4]
+            jj = j % 4
+            for g in range(G):
+                nc.tensor.matmul_mx(
+                    out=acc[:],
+                    lhsT=codes[:, a, g, :].bitcast(FP8X4),
+                    lhsT_scale=hsc[:, a, g, :],
+                    rhs=w[:, g, 1024 * jj : 1024 * (jj + 1)].bitcast(FP4X4),
+                    rhs_scale=wsc[:, g, 512 * j : 512 * (j + 1)],
+                    start=(g == 0),
+                    stop=(g == G - 1),
+                )
+            return acc
+
+        transposes(0)
+        for step in prep_steps(0):
+            step()
+        transposes(1)
+
+        for a in range(NT):
+            o = stage.tile([P, SC], F32, name="o")
+            cur = cur_tiles[a]
+            steps = prep_steps(a + 1) if a + 1 < NT else []
+            done = 0
+            for idx, j in enumerate(BANK_ORDER):
+                cols = slice(512 * j, 512 * (j + 1))
+                acc = product(a, j)
+                if j in VECTOR_BANKS:
+                    nc.vector.tensor_tensor(out=o[:, cols], in0=acc[:], in1=cur[:, cols], op=ALU.add)
+                    if done < len(steps):
+                        steps[done]()
+                        done += 1
+                else:
+                    nc.scalar.copy(out=o[:, cols], in_=acc[:])
+                if idx % 4 == 3:
+                    half = idx // 4
+                    gcols = slice(2048 * half + 1024, 2048 * half + 2048)
+                    nc.gpsimd.tensor_tensor(out=o[:, gcols], in0=o[:, gcols], in1=cur[:, gcols], op=ALU.add)
+                    hcols = slice(2048 * half, 2048 * (half + 1))
+                    nc.sync.dma_start(out=out_v[:, a, hcols], in_=o[:, hcols])
+            if a + 2 < NT:
+                transposes(a + 2)

@@ -20,10 +20,8 @@ NB = SC // 512
 
 FLOPS = 2 * S * B * SC
 
-P_UNITS = ((0,), (1,), (2, 3), (4, 5, 6, 7))
-CUR_UNITS = ((0,), (1,), (2, 3), (4, 5), (6, 7))
-VECTOR_BANKS = (0, 1, 4, 5)
-BANK_ORDER = (0, 2, 1, 3, 4, 6, 5, 7)
+PLAN_BODY = ((0, "v"), (2, "s"), (1, "v"), (3, "s"), (4, "v"), (6, "s"), (5, "v"), (7, "s"))
+PLAN_LAST = ((0, "s"), (1, "s"), (2, "v"), (3, "v"), (4, "v"), (5, "v"), (6, "v"), (7, "v"))
 
 
 def tile_optblockv2_kernel(
@@ -39,9 +37,11 @@ def tile_optblockv2_kernel(
     with ExitStack() as ctx:
         keep = ctx.enter_context(tc.tile_pool(name="keep", bufs=1))
         work = ctx.enter_context(tc.tile_pool(name="work", bufs=2))
-        stage = ctx.enter_context(tc.tile_pool(name="stage", bufs=5))
+        stage = ctx.enter_context(tc.tile_pool(name="stage", bufs=6))
+        sorted_pool = ctx.enter_context(tc.tile_pool(name="sorted_pool", bufs=3))
         tpool = ctx.enter_context(tc.psum_pool(name="tpool", bufs=2))
         apool = ctx.enter_context(tc.psum_pool(name="apool", bufs=6))
+        ctx.enter_context(tc.manual_schedule())
 
         wsc = keep.tile([P, G, SC], U8, name="wsc", align_bytes=64)
         nc.vector.memset(wsc[:].bitcast(I32), 0)
@@ -59,13 +59,18 @@ def tile_optblockv2_kernel(
             for i, a in enumerate(unit):
                 p_tiles[a] = t[:, i, :]
 
-        def load_cur(unit):
-            t = keep.tile([P, len(unit), SC], BF16, name="cur%d" % unit[0])
-            nc.sync.dma_start(out=t[:], in_=cur_v[:, unit[0] : unit[-1] + 1, :])
+        def load_cur(unit, n0=0, n1=SC):
+            t = keep.tile([P, len(unit), n1 - n0], BF16, name="cur%d_%d" % (unit[0], n0))
+            nc.sync.dma_start(out=t[:], in_=cur_v[:, unit[0] : unit[-1] + 1, n0:n1])
             for i, a in enumerate(unit):
-                cur_tiles[a] = t[:, i, :]
+                for n in range(n0, n1, 512):
+                    cur_tiles[(a, n)] = (t[:, i, :], n - n0)
 
-        load_p(P_UNITS[0])
+        def cur_cols(a, n0, n1):
+            part, start = cur_tiles[(a, n0)]
+            return part[:, start : start + n1 - n0]
+
+        load_p((0, 1))
         nc.scalar.dma_start(
             out=av_raw[:], in_=avail_bundle.rearrange("(g p t) -> p g t", g=G, p=P, t=4)
         )
@@ -76,20 +81,24 @@ def tile_optblockv2_kernel(
         for r in range(4):
             nc.sync.dma_start(out=wsc_i[r:P:32, :, :], in_=scales_v[r])
         w_tiles = []
-        for c in range(2):
+
+        def load_words(c):
             w = keep.tile([P, G, SC], U8, name="w%d" % c, align_bytes=64)
             nc.sync.dma_start(
                 out=w[:].bitcast(I32), in_=words_v[:, :, 1024 * c : 1024 * (c + 1)]
             )
             w_tiles.append(w)
-        load_cur(CUR_UNITS[0])
-        load_p(P_UNITS[1])
-        load_cur(CUR_UNITS[1])
-        load_p(P_UNITS[2])
-        load_cur(CUR_UNITS[2])
-        load_p(P_UNITS[3])
-        load_cur(CUR_UNITS[3])
-        load_cur(CUR_UNITS[4])
+
+        load_words(0)
+        load_cur((0,), 0, 2048)
+        load_words(1)
+        load_cur((0,), 2048, 4096)
+        load_p((2, 3))
+        load_cur((1,))
+        load_cur((2, 3))
+        load_p((4, 5, 6, 7))
+        load_cur((4, 5))
+        load_cur((6, 7))
 
         hi = keep.tile([P, G * 4], F32, name="hi")
         lo = keep.tile([P, G * 4], F32, name="lo")
@@ -106,16 +115,24 @@ def tile_optblockv2_kernel(
         hsc = keep.tile([P, NT, G, P], U8, name="hsc", align_bytes=64)
 
         tps = {}
+        sorted_p = {}
+
+        def sort_columns(a):
+            ps = sorted_pool.tile([P, G, 4, P], BF16, name="ps")
+            nc.scalar.copy(
+                out=ps[:], in_=p_tiles[a].rearrange("s (g p t) -> s g t p", g=G, p=P, t=4)
+            )
+            sorted_p[a] = ps
 
         def transposes(a):
             tp = tpool.tile([P, G * 4, P], BF16, name="tp")
             for g in range(G):
                 for t in range(4):
-                    nc.tensor.transpose(
-                        tp[:, 4 * g + t, :],
-                        p_tiles[a][:, 512 * g + t : 512 * (g + 1) : 4],
-                        ident[:],
-                    )
+                    if a in sorted_p:
+                        columns = sorted_p[a][:, g, t, :]
+                    else:
+                        columns = p_tiles[a][:, 512 * g + t : 512 * (g + 1) : 4]
+                    nc.tensor.transpose(tp[:, 4 * g + t, :], columns, ident[:])
             tps[a] = tp
 
         def prep_steps(a):
@@ -175,30 +192,51 @@ def tile_optblockv2_kernel(
             return acc
 
         transposes(0)
+        sort_columns(1)
         for step in prep_steps(0):
             step()
         transposes(1)
 
         for a in range(NT):
             o = stage.tile([P, SC], F32, name="o")
-            cur = cur_tiles[a]
-            steps = prep_steps(a + 1) if a + 1 < NT else []
+            last = a == NT - 1
+            plan = PLAN_LAST if last else PLAN_BODY
+            steps = prep_steps(a + 1) if not last else []
             done = 0
-            for idx, j in enumerate(BANK_ORDER):
+            if steps:
+                steps[0]()
+                done = 1
+            for pos, (j, engine) in enumerate(plan):
                 cols = slice(512 * j, 512 * (j + 1))
                 acc = product(a, j)
-                if j in VECTOR_BANKS:
-                    nc.vector.tensor_tensor(out=o[:, cols], in0=acc[:], in1=cur[:, cols], op=ALU.add)
+                if engine == "v":
+                    nc.vector.tensor_tensor(
+                        out=o[:, cols], in0=acc[:], in1=cur_cols(a, 512 * j, 512 * (j + 1)), op=ALU.add
+                    )
                     if done < len(steps):
                         steps[done]()
                         done += 1
                 else:
                     nc.scalar.copy(out=o[:, cols], in_=acc[:])
-                if idx % 4 == 3:
-                    half = idx // 4
-                    gcols = slice(2048 * half + 1024, 2048 * half + 2048)
-                    nc.gpsimd.tensor_tensor(out=o[:, gcols], in0=o[:, gcols], in1=cur[:, gcols], op=ALU.add)
-                    hcols = slice(2048 * half, 2048 * (half + 1))
-                    nc.sync.dma_start(out=out_v[:, a, hcols], in_=o[:, hcols])
+                    if j % 2 == 1:
+                        pair = slice(512 * (j - 1), 512 * (j + 1))
+                        nc.gpsimd.tensor_tensor(
+                            out=o[:, pair], in0=o[:, pair],
+                            in1=cur_cols(a, 512 * (j - 1), 512 * (j + 1)), op=ALU.add,
+                        )
+                if pos == 3 and a + 2 < NT:
+                    sort_columns(a + 2)
+                if last and pos in (3, 5):
+                    quarter = slice(1024 * (pos // 2), 1024 * (pos // 2 + 1))
+                    nc.sync.dma_start(out=out_v[:, a, quarter], in_=o[:, quarter])
+                if a == NT - 2 and pos == 3:
+                    nc.sync.dma_start(out=out_v[:, a, 0:2048], in_=o[:, 0:2048])
+            if last:
+                nc.sync.dma_start(out=out_v[:, a, 0:1024], in_=o[:, 0:1024])
+                nc.sync.dma_start(out=out_v[:, a, 3072:4096], in_=o[:, 3072:4096])
+            elif a == NT - 2:
+                nc.sync.dma_start(out=out_v[:, a, 2048:4096], in_=o[:, 2048:4096])
+            else:
+                nc.sync.dma_start(out=out_v[:, a, :], in_=o[:])
             if a + 2 < NT:
                 transposes(a + 2)

@@ -32,7 +32,7 @@ def tile_optblockv2_kernel(
     cur_v = cur_inven.rearrange("(p a) n -> p a n", a=NT)
     out_v = out.rearrange("o (p a n) -> (o p) a n", p=P, a=NT, n=SC)
     words_v = bun_sc_words.bitcast(I32).rearrange("g p w -> p g w")
-    scales_v = bun_sc_scales.bitcast(I32).rearrange("g (q r) w -> r q g w", r=4)
+    scales_v = bun_sc_scales.bitcast(F32).rearrange("g (q r) w -> r q g w", r=4)
 
     with ExitStack() as ctx:
         keep = ctx.enter_context(tc.tile_pool(name="keep", bufs=1))
@@ -77,9 +77,9 @@ def tile_optblockv2_kernel(
         nc.scalar.dma_start(
             out=al_raw[:], in_=alloc_bundle.rearrange("(g p t) -> p g t", g=G, p=P, t=4)
         )
-        wsc_i = wsc[:].bitcast(I32)
+        wsc_f = wsc[:].bitcast(F32)
         for r in range(4):
-            nc.sync.dma_start(out=wsc_i[r:P:32, :, :], in_=scales_v[r])
+            nc.gpsimd.dma_start(out=wsc_f[r:P:32, :, :], in_=scales_v[r])
         w_tiles = []
 
         def load_words(c):

@@ -32,7 +32,7 @@ def tile_optblockv2_kernel(
     cur_v = cur_inven.rearrange("(p a) n -> p a n", a=NT)
     out_v = out.rearrange("o (p a n) -> (o p) a n", p=P, a=NT, n=SC)
     words_v = bun_sc_words.bitcast(I32).rearrange("g p w -> p g w")
-    scales_v = bun_sc_scales.bitcast(F32).rearrange("g (q r) w -> r q g w", r=4)
+    scales_v = bun_sc_scales.bitcast(I32).rearrange("g (q r) w -> r q g w", r=4)
 
     with ExitStack() as ctx:
         keep = ctx.enter_context(tc.tile_pool(name="keep", bufs=1))
@@ -77,9 +77,9 @@ def tile_optblockv2_kernel(
         nc.scalar.dma_start(
             out=al_raw[:], in_=alloc_bundle.rearrange("(g p t) -> p g t", g=G, p=P, t=4)
         )
-        wsc_f = wsc[:].bitcast(F32)
+        wsc_i = wsc[:].bitcast(I32)
         for r in range(4):
-            nc.gpsimd.dma_start(out=wsc_f[r:P:32, :, :], in_=scales_v[r])
+            nc.sync.dma_start(out=wsc_i[r:P:32, :, :], in_=scales_v[r])
         w_tiles = []
 
         def load_words(c):
@@ -90,10 +90,10 @@ def tile_optblockv2_kernel(
             w_tiles.append(w)
 
         load_words(0)
+        load_p((2, 3))
         load_cur((0,), 0, 2048)
         load_words(1)
         load_cur((0,), 2048, 4096)
-        load_p((2, 3))
         load_cur((1,))
         load_cur((2, 3))
         load_p((4, 5, 6, 7))
@@ -193,19 +193,21 @@ def tile_optblockv2_kernel(
 
         transposes(0)
         sort_columns(1)
+        sort_columns(2)
         for step in prep_steps(0):
             step()
         transposes(1)
+        pending = prep_steps(1)
+        written = 0
 
         for a in range(NT):
             o = stage.tile([P, SC], F32, name="o")
             last = a == NT - 1
             plan = PLAN_LAST if last else PLAN_BODY
-            steps = prep_steps(a + 1) if not last else []
-            done = 0
-            if steps:
-                steps[0]()
-                done = 1
+            if a == 0:
+                pending[0]()
+                pending[1]()
+                written = 2
             for pos, (j, engine) in enumerate(plan):
                 cols = slice(512 * j, 512 * (j + 1))
                 acc = product(a, j)
@@ -213,9 +215,9 @@ def tile_optblockv2_kernel(
                     nc.vector.tensor_tensor(
                         out=o[:, cols], in0=acc[:], in1=cur_cols(a, 512 * j, 512 * (j + 1)), op=ALU.add
                     )
-                    if done < len(steps):
-                        steps[done]()
-                        done += 1
+                    if written < len(pending):
+                        pending[written]()
+                        written += 1
                 else:
                     nc.scalar.copy(out=o[:, cols], in_=acc[:])
                     if j % 2 == 1:
@@ -225,18 +227,21 @@ def tile_optblockv2_kernel(
                             in1=cur_cols(a, 512 * (j - 1), 512 * (j + 1)), op=ALU.add,
                         )
                 if pos == 3 and a + 2 < NT:
-                    sort_columns(a + 2)
+                    transposes(a + 2)
+                    pending.extend(prep_steps(a + 2))
+                if pos == 5 and a + 3 < NT:
+                    sort_columns(a + 3)
                 if last and pos in (3, 5):
                     quarter = slice(1024 * (pos // 2), 1024 * (pos // 2 + 1))
                     nc.sync.dma_start(out=out_v[:, a, quarter], in_=o[:, quarter])
+                if last and pos == 6:
+                    nc.sync.dma_start(out=out_v[:, a, cols], in_=o[:, cols])
+                    nc.sync.dma_start(out=out_v[:, a, 0:1024], in_=o[:, 0:1024])
+                if last and pos == 7:
+                    nc.sync.dma_start(out=out_v[:, a, cols], in_=o[:, cols])
                 if a == NT - 2 and pos == 3:
                     nc.sync.dma_start(out=out_v[:, a, 0:2048], in_=o[:, 0:2048])
-            if last:
-                nc.sync.dma_start(out=out_v[:, a, 0:1024], in_=o[:, 0:1024])
-                nc.sync.dma_start(out=out_v[:, a, 3072:4096], in_=o[:, 3072:4096])
-            elif a == NT - 2:
+            if a == NT - 2:
                 nc.sync.dma_start(out=out_v[:, a, 2048:4096], in_=o[:, 2048:4096])
-            else:
+            elif not last:
                 nc.sync.dma_start(out=out_v[:, a, :], in_=o[:])
-            if a + 2 < NT:
-                transposes(a + 2)

@@ -78,8 +78,6 @@ def tile_optblockv2_kernel(
             out=al_raw[:], in_=alloc_bundle.rearrange("(g p t) -> p g t", g=G, p=P, t=4)
         )
         wsc_i = wsc[:].bitcast(I32)
-        for r in range(4):
-            nc.sync.dma_start(out=wsc_i[r:P:32, :, :], in_=scales_v[r])
         w_tiles = []
 
         def load_words(c):
@@ -90,6 +88,8 @@ def tile_optblockv2_kernel(
             w_tiles.append(w)
 
         load_words(0)
+        for r in range(4):
+            nc.sync.dma_start(out=wsc_i[r:P:32, :, :], in_=scales_v[r])
         load_p((2, 3))
         load_cur((0,), 0, 2048)
         load_words(1)

@@ -43,9 +43,9 @@ def tile_optblockv2_kernel(
         apool = ctx.enter_context(tc.psum_pool(name="apool", bufs=6))
         ctx.enter_context(tc.manual_schedule())
 
-        wsc = keep.tile([P, G, SC], U8, name="wsc", align_bytes=64)
+        wsc = keep.tile([P, G, SC], U8, name="wsc", align_bytes=256)
         nc.vector.memset(wsc[:].bitcast(I32), 0)
-        ident = keep.tile([P, P], BF16, name="ident")
+        ident = keep.tile([P, P], BF16, name="ident", align_bytes=256)
         make_identity(nc, ident[:])
 
         av_raw = keep.tile([P, G, 4], BF16, name="av_raw")
@@ -54,13 +54,13 @@ def tile_optblockv2_kernel(
         cur_tiles = {}
 
         def load_p(unit):
-            t = keep.tile([P, len(unit), B], BF16, name="p%d" % unit[0])
+            t = keep.tile([P, len(unit), B], BF16, name="p%d" % unit[0], align_bytes=256)
             nc.sync.dma_start(out=t[:], in_=p_v[:, unit[0] : unit[-1] + 1, :])
             for i, a in enumerate(unit):
                 p_tiles[a] = t[:, i, :]
 
         def load_cur(unit, n0=0, n1=SC):
-            t = keep.tile([P, len(unit), n1 - n0], BF16, name="cur%d_%d" % (unit[0], n0))
+            t = keep.tile([P, len(unit), n1 - n0], BF16, name="cur%d_%d" % (unit[0], n0), align_bytes=256)
             nc.sync.dma_start(out=t[:], in_=cur_v[:, unit[0] : unit[-1] + 1, n0:n1])
             for i, a in enumerate(unit):
                 for n in range(n0, n1, 512):
@@ -81,7 +81,7 @@ def tile_optblockv2_kernel(
         w_tiles = []
 
         def load_words(c):
-            w = keep.tile([P, G, SC], U8, name="w%d" % c, align_bytes=64)
+            w = keep.tile([P, G, SC], U8, name="w%d" % c, align_bytes=256)
             nc.sync.dma_start(
                 out=w[:].bitcast(I32), in_=words_v[:, :, 1024 * c : 1024 * (c + 1)]
             )
@@ -111,14 +111,14 @@ def tile_optblockv2_kernel(
             scalar1=-1.0, scalar2=0.0, op0=ALU.mult, op1=ALU.min,
         )
 
-        codes = keep.tile([P, NT, G, P], U32, name="codes", align_bytes=64)
-        hsc = keep.tile([P, NT, G, P], U8, name="hsc", align_bytes=64)
+        codes = keep.tile([P, NT, G, P], U32, name="codes", align_bytes=256)
+        hsc = keep.tile([P, NT, G, P], U8, name="hsc", align_bytes=256)
 
         tps = {}
         sorted_p = {}
 
         def sort_columns(a):
-            ps = sorted_pool.tile([P, G, 4, P], BF16, name="ps")
+            ps = sorted_pool.tile([P, G, 4, P], BF16, name="ps", align_bytes=256)
             nc.scalar.copy(
                 out=ps[:], in_=p_tiles[a].rearrange("s (g p t) -> s g t p", g=G, p=P, t=4)
             )
@@ -137,9 +137,9 @@ def tile_optblockv2_kernel(
 
         def prep_steps(a):
             tp = tps[a]
-            r = work.tile([P, G * 4, P], BF16, name="r")
-            m = work.tile([P, G * 4, P], BF16, name="m")
-            hg = work.tile([P, G, P, 4], BF16, name="hg", align_bytes=64)
+            r = work.tile([P, G * 4, P], BF16, name="r", align_bytes=256)
+            m = work.tile([P, G * 4, P], BF16, name="m", align_bytes=256)
+            hg = work.tile([P, G, P, 4], BF16, name="hg", align_bytes=256)
 
             def clamp(q0, q1):
                 for q in range(q0, q1):
@@ -201,7 +201,7 @@ def tile_optblockv2_kernel(
         written = 0
 
         for a in range(NT):
-            o = stage.tile([P, SC], F32, name="o")
+            o = stage.tile([P, SC], F32, name="o", align_bytes=256)
             last = a == NT - 1
             plan = PLAN_LAST if last else PLAN_BODY
             if a == 0:

@@ -37,7 +37,7 @@ def tile_optblockv2_kernel(
     with ExitStack() as ctx:
         keep = ctx.enter_context(tc.tile_pool(name="keep", bufs=1))
         work = ctx.enter_context(tc.tile_pool(name="work", bufs=2))
-        stage = ctx.enter_context(tc.tile_pool(name="stage", bufs=6))
+        stage = ctx.enter_context(tc.tile_pool(name="stage", bufs=3))
         sorted_pool = ctx.enter_context(tc.tile_pool(name="sorted_pool", bufs=3))
         tpool = ctx.enter_context(tc.psum_pool(name="tpool", bufs=2))
         apool = ctx.enter_context(tc.psum_pool(name="apool", bufs=6))
@@ -97,8 +97,7 @@ def tile_optblockv2_kernel(
         load_cur((1,))
         load_cur((2, 3))
         load_p((4, 5, 6, 7))
-        load_cur((4, 5))
-        load_cur((6, 7))
+        load_cur((4, 5, 6, 7))
 
         hi = keep.tile([P, G * 4], F32, name="hi")
         lo = keep.tile([P, G * 4], F32, name="lo")
@@ -201,7 +200,9 @@ def tile_optblockv2_kernel(
         written = 0
 
         for a in range(NT):
-            o = stage.tile([P, SC], F32, name="o", align_bytes=256)
+            if a % 2 == 0:
+                two_tiles = stage.tile([P, 2, SC], F32, name="two_tiles", align_bytes=256)
+            o = two_tiles[:, a % 2, :]
             last = a == NT - 1
             plan = PLAN_LAST if last else PLAN_BODY
             if a == 0:
@@ -231,17 +232,11 @@ def tile_optblockv2_kernel(
                     pending.extend(prep_steps(a + 2))
                 if pos == 5 and a + 3 < NT:
                     sort_columns(a + 3)
-                if last and pos in (3, 5):
-                    quarter = slice(1024 * (pos // 2), 1024 * (pos // 2 + 1))
-                    nc.sync.dma_start(out=out_v[:, a, quarter], in_=o[:, quarter])
-                if last and pos == 6:
-                    nc.sync.dma_start(out=out_v[:, a, cols], in_=o[:, cols])
-                    nc.sync.dma_start(out=out_v[:, a, 0:1024], in_=o[:, 0:1024])
-                if last and pos == 7:
-                    nc.sync.dma_start(out=out_v[:, a, cols], in_=o[:, cols])
-                if a == NT - 2 and pos == 3:
+                if last and pos == 5:
                     nc.sync.dma_start(out=out_v[:, a, 0:2048], in_=o[:, 0:2048])
-            if a == NT - 2:
-                nc.sync.dma_start(out=out_v[:, a, 2048:4096], in_=o[:, 2048:4096])
-            elif not last:
-                nc.sync.dma_start(out=out_v[:, a, :], in_=o[:])
+                if last and pos == 7:
+                    nc.sync.dma_start(out=out_v[:, a, 2048:4096], in_=o[:, 2048:4096])
+            if a == 1:
+                nc.sync.dma_start(out=out_v[:, 0:2, :], in_=two_tiles[:])
+            elif a != 0 and not last:
+                nc.sync.dma_start(out=out_v[:, a, :], in_=o)

@@ -44,12 +44,12 @@ def tile_optblockv2_kernel(
         ctx.enter_context(tc.manual_schedule())
 
         wsc = keep.tile([P, G, SC], U8, name="wsc", align_bytes=256)
+        bounds = keep.tile([P, 512], BF16, name="bounds", align_bytes=256)
+        nc.vector.memset(bounds[:].bitcast(F32), 0.0)
         nc.vector.memset(wsc[:].bitcast(I32), 0)
         ident = keep.tile([P, P], BF16, name="ident", align_bytes=256)
         make_identity(nc, ident[:])
 
-        av_raw = keep.tile([P, G, 4], BF16, name="av_raw")
-        al_raw = keep.tile([P, G, 4], BF16, name="al_raw")
         p_tiles = {}
         cur_tiles = {}
 
@@ -71,12 +71,8 @@ def tile_optblockv2_kernel(
             return part[:, start : start + n1 - n0]
 
         load_p((0, 1))
-        nc.scalar.dma_start(
-            out=av_raw[:], in_=avail_bundle.rearrange("(g p t) -> p g t", g=G, p=P, t=4)
-        )
-        nc.scalar.dma_start(
-            out=al_raw[:], in_=alloc_bundle.rearrange("(g p t) -> p g t", g=G, p=P, t=4)
-        )
+        nc.scalar.dma_start(out=bounds[0:2, :], in_=avail_bundle.rearrange("(g k) -> g k", g=G))
+        nc.scalar.dma_start(out=bounds[2:4, :], in_=alloc_bundle.rearrange("(g k) -> g k", g=G))
         wsc_i = wsc[:].bitcast(I32)
         w_tiles = []
 
@@ -101,14 +97,6 @@ def tile_optblockv2_kernel(
 
         hi = keep.tile([P, G * 4], F32, name="hi")
         lo = keep.tile([P, G * 4], F32, name="lo")
-        nc.vector.tensor_scalar(
-            out=hi[:], in0=av_raw[:].rearrange("p g t -> p (g t)"),
-            scalar1=0.0, scalar2=None, op0=ALU.max,
-        )
-        nc.vector.tensor_scalar(
-            out=lo[:], in0=al_raw[:].rearrange("p g t -> p (g t)"),
-            scalar1=-1.0, scalar2=0.0, op0=ALU.mult, op1=ALU.min,
-        )
 
         codes = keep.tile([P, NT, G, P], U32, name="codes", align_bytes=256)
         hsc = keep.tile([P, NT, G, P], U8, name="hsc", align_bytes=256)
@@ -191,6 +179,19 @@ def tile_optblockv2_kernel(
             return acc
 
         transposes(0)
+        bt = tpool.tile([P, G * 4, P], BF16, name="tp")
+        for t in range(4):
+            nc.tensor.transpose(bt[:, t, :], bounds[:, t:512:4], ident[:])
+        nc.vector.tensor_scalar(
+            out=hi[:].rearrange("p (g t) -> p g t", g=G),
+            in0=bt[:, 0:4, 0:2].rearrange("p t g -> p g t"),
+            scalar1=0.0, scalar2=None, op0=ALU.max,
+        )
+        nc.vector.tensor_scalar(
+            out=lo[:].rearrange("p (g t) -> p g t", g=G),
+            in0=bt[:, 0:4, 2:4].rearrange("p t g -> p g t"),
+            scalar1=-1.0, scalar2=0.0, op0=ALU.mult, op1=ALU.min,
+        )
         sort_columns(1)
         sort_columns(2)
         for step in prep_steps(0):

@@ -28,9 +28,9 @@ def tile_optblockv2_kernel(
     tc, proba, cur_inven, bun_sc_words, bun_sc_scales, avail_bundle, alloc_bundle, out
 ):
     nc = tc.nc
-    p_v = proba.rearrange("(p a k) -> p a k", p=P, a=NT, k=B)
-    cur_v = cur_inven.rearrange("(p a) n -> p a n", a=NT)
-    out_v = out.rearrange("o (p a n) -> (o p) a n", p=P, a=NT, n=SC)
+    p_v = proba.rearrange("(u p v k) -> p u v k", u=NT // 2, p=P, v=2, k=B)
+    cur_v = cur_inven.rearrange("(u p v) n -> p u v n", u=NT // 2, v=2)
+    out_v = out.rearrange("o (u p v n) -> (o p) u v n", u=NT // 2, p=P, v=2, n=SC)
     words_v = bun_sc_words.bitcast(I32).rearrange("g p w -> p g w")
     scales_v = bun_sc_scales.bitcast(I32).rearrange("g (q r) w -> r q g w", r=4)
 
@@ -55,13 +55,22 @@ def tile_optblockv2_kernel(
 
         def load_p(unit):
             t = keep.tile([P, len(unit), B], BF16, name="p%d" % unit[0], align_bytes=256)
-            nc.sync.dma_start(out=t[:], in_=p_v[:, unit[0] : unit[-1] + 1, :])
+            nc.sync.dma_start(
+                out=t[:].rearrange("p (u v) k -> p u v k", v=2),
+                in_=p_v[:, unit[0] // 2 : unit[-1] // 2 + 1, :, :],
+            )
             for i, a in enumerate(unit):
                 p_tiles[a] = t[:, i, :]
 
         def load_cur(unit, n0=0, n1=SC):
             t = keep.tile([P, len(unit), n1 - n0], BF16, name="cur%d_%d" % (unit[0], n0), align_bytes=256)
-            nc.sync.dma_start(out=t[:], in_=cur_v[:, unit[0] : unit[-1] + 1, n0:n1])
+            if len(unit) == 1:
+                nc.sync.dma_start(out=t[:, 0, :], in_=cur_v[:, unit[0] // 2, unit[0] % 2, n0:n1])
+            else:
+                nc.sync.dma_start(
+                    out=t[:].rearrange("p (u v) n -> p u v n", v=2),
+                    in_=cur_v[:, unit[0] // 2 : unit[-1] // 2 + 1, :, n0:n1],
+                )
             for i, a in enumerate(unit):
                 for n in range(n0, n1, 512):
                     cur_tiles[(a, n)] = (t[:, i, :], n - n0)
@@ -234,10 +243,10 @@ def tile_optblockv2_kernel(
                 if pos == 5 and a + 3 < NT:
                     sort_columns(a + 3)
                 if last and pos == 5:
-                    nc.sync.dma_start(out=out_v[:, a, 0:2048], in_=o[:, 0:2048])
+                    nc.sync.dma_start(out=out_v[:, a // 2, a % 2, 0:2048], in_=o[:, 0:2048])
                 if last and pos == 7:
-                    nc.sync.dma_start(out=out_v[:, a, 2048:4096], in_=o[:, 2048:4096])
+                    nc.sync.dma_start(out=out_v[:, a // 2, a % 2, 2048:4096], in_=o[:, 2048:4096])
             if a == 1:
-                nc.sync.dma_start(out=out_v[:, 0:2, :], in_=two_tiles[:])
+                nc.sync.dma_start(out=out_v[:, 0, :, :], in_=two_tiles[:])
             elif a != 0 and not last:
-                nc.sync.dma_start(out=out_v[:, a, :], in_=o)
+                nc.sync.dma_start(out=out_v[:, a // 2, a % 2, :], in_=o)

@@ -80,8 +80,8 @@ def tile_optblockv2_kernel(
             return part[:, start : start + n1 - n0]
 
         load_p((0, 1))
-        nc.scalar.dma_start(out=bounds[0:2, :], in_=avail_bundle.rearrange("(g k) -> g k", g=G))
-        nc.scalar.dma_start(out=bounds[2:4, :], in_=alloc_bundle.rearrange("(g k) -> g k", g=G))
+        nc.scalar.dma_start(out=bounds[8:10, :], in_=avail_bundle.rearrange("(g k) -> g k", g=G))
+        nc.scalar.dma_start(out=bounds[10:12, :], in_=alloc_bundle.rearrange("(g k) -> g k", g=G))
         wsc_i = wsc[:].bitcast(I32)
         w_tiles = []
 
@@ -95,8 +95,8 @@ def tile_optblockv2_kernel(
         load_words(0)
         for r in range(4):
             nc.sync.dma_start(out=wsc_i[r:P:32, :, :], in_=scales_v[r])
-        load_p((2, 3))
         load_cur((0,), 0, 2048)
+        load_p((2, 3))
         load_words(1)
         load_cur((0,), 2048, 4096)
         load_cur((1,))
@@ -115,9 +115,13 @@ def tile_optblockv2_kernel(
 
         def sort_columns(a):
             ps = sorted_pool.tile([P, G, 4, P], BF16, name="ps", align_bytes=256)
-            nc.scalar.copy(
-                out=ps[:], in_=p_tiles[a].rearrange("s (g p t) -> s g t p", g=G, p=P, t=4)
-            )
+            columns = p_tiles[a].rearrange("s (g p t) -> s g t p", g=G, p=P, t=4)
+            if a == 2:
+                nc.gpsimd.tensor_scalar(
+                    out=ps[:], in0=columns, scalar1=1.0, scalar2=0.0, op0=ALU.mult, op1=ALU.add
+                )
+            else:
+                nc.scalar.copy(out=ps[:], in_=columns)
             sorted_p[a] = ps
 
         def transposes(a):
@@ -193,12 +197,12 @@ def tile_optblockv2_kernel(
             nc.tensor.transpose(bt[:, t, :], bounds[:, t:512:4], ident[:])
         nc.vector.tensor_scalar(
             out=hi[:].rearrange("p (g t) -> p g t", g=G),
-            in0=bt[:, 0:4, 0:2].rearrange("p t g -> p g t"),
+            in0=bt[:, 0:4, 8:10].rearrange("p t g -> p g t"),
             scalar1=0.0, scalar2=None, op0=ALU.max,
         )
         nc.vector.tensor_scalar(
             out=lo[:].rearrange("p (g t) -> p g t", g=G),
-            in0=bt[:, 0:4, 2:4].rearrange("p t g -> p g t"),
+            in0=bt[:, 0:4, 10:12].rearrange("p t g -> p g t"),
             scalar1=-1.0, scalar2=0.0, op0=ALU.mult, op1=ALU.min,
         )
         sort_columns(1)
@@ -226,9 +230,10 @@ def tile_optblockv2_kernel(
                     nc.vector.tensor_tensor(
                         out=o[:, cols], in0=acc[:], in1=cur_cols(a, 512 * j, 512 * (j + 1)), op=ALU.add
                     )
-                    if written < len(pending):
-                        pending[written]()
-                        written += 1
+                    for step in range(2 if a == 1 and pos == 0 else 1):
+                        if written < len(pending):
+                            pending[written]()
+                            written += 1
                 else:
                     nc.scalar.copy(out=o[:, cols], in_=acc[:])
                     if j % 2 == 1:
@@ -237,7 +242,7 @@ def tile_optblockv2_kernel(
                             out=o[:, pair], in0=o[:, pair],
                             in1=cur_cols(a, 512 * (j - 1), 512 * (j + 1)), op=ALU.add,
                         )
-                if pos == 3 and a + 2 < NT:
+                if pos == (5 if a == 0 else 3) and a + 2 < NT:
                     transposes(a + 2)
                     pending.extend(prep_steps(a + 2))
                 if pos == 5 and a + 3 < NT:

from contextlib import ExitStack

import concourse.mybir as mybir
from concourse.masks import make_identity

BF16 = mybir.dt.bfloat16
F32 = mybir.dt.float32
I32 = mybir.dt.int32
U8 = mybir.dt.uint8
U32 = mybir.dt.uint32
FP8X4 = mybir.dt.float8_e4m3fn_x4
FP4X4 = mybir.dt.float4_e2m1fn_x4
ALU = mybir.AluOpType

P = 128
S, B, SC = 1024, 1024, 4096
NT = S // P
G = B // 512
NB = SC // 512

FLOPS = 2 * S * B * SC

PLAN_BODY = ((0, "v"), (2, "s"), (1, "v"), (3, "s"), (4, "v"), (6, "s"), (5, "v"), (7, "s"))
PLAN_LAST = ((0, "s"), (1, "s"), (2, "v"), (3, "v"), (4, "v"), (5, "v"), (6, "v"), (7, "v"))


def tile_optblockv2_kernel(
    tc, proba, cur_inven, bun_sc_words, bun_sc_scales, avail_bundle, alloc_bundle, out
):
    nc = tc.nc
    p_v = proba.rearrange("(u p v k) -> p u v k", u=NT // 2, p=P, v=2, k=B)
    cur_v = cur_inven.rearrange("(u p v) n -> p u v n", u=NT // 2, v=2)
    out_v = out.rearrange("o (u p v n) -> (o p) u v n", u=NT // 2, p=P, v=2, n=SC)
    words_v = bun_sc_words.bitcast(I32).rearrange("g p w -> p g w")
    scales_v = bun_sc_scales.bitcast(I32).rearrange("g (q r) w -> r q g w", r=4)

    with ExitStack() as ctx:
        keep = ctx.enter_context(tc.tile_pool(name="keep", bufs=1))
        work = ctx.enter_context(tc.tile_pool(name="work", bufs=2))
        stage = ctx.enter_context(tc.tile_pool(name="stage", bufs=3))
        sorted_pool = ctx.enter_context(tc.tile_pool(name="sorted_pool", bufs=3))
        tpool = ctx.enter_context(tc.psum_pool(name="tpool", bufs=2))
        apool = ctx.enter_context(tc.psum_pool(name="apool", bufs=6))
        ctx.enter_context(tc.manual_schedule())

        wsc = keep.tile([P, G, SC], U8, name="wsc", align_bytes=256)
        bounds = keep.tile([P, 512], BF16, name="bounds", align_bytes=256)
        nc.vector.memset(bounds[:].bitcast(F32), 0.0)
        nc.vector.memset(wsc[:].bitcast(I32), 0)
        ident = keep.tile([P, P], BF16, name="ident", align_bytes=256)
        make_identity(nc, ident[:])

        p_tiles = {}
        cur_tiles = {}

        def load_p(unit):
            t = keep.tile([P, len(unit), B], BF16, name="p%d" % unit[0], align_bytes=256)
            nc.sync.dma_start(
                out=t[:].rearrange("p (u v) k -> p u v k", v=2),
                in_=p_v[:, unit[0] // 2 : unit[-1] // 2 + 1, :, :],
            )
            for i, a in enumerate(unit):
                p_tiles[a] = t[:, i, :]

        def load_cur(unit, n0=0, n1=SC):
            t = keep.tile([P, len(unit), n1 - n0], BF16, name="cur%d_%d" % (unit[0], n0), align_bytes=256)
            if len(unit) == 1:
                nc.sync.dma_start(out=t[:, 0, :], in_=cur_v[:, unit[0] // 2, unit[0] % 2, n0:n1])
            else:
                nc.sync.dma_start(
                    out=t[:].rearrange("p (u v) n -> p u v n", v=2),
                    in_=cur_v[:, unit[0] // 2 : unit[-1] // 2 + 1, :, n0:n1],
                )
            for i, a in enumerate(unit):
                for n in range(n0, n1, 512):
                    cur_tiles[(a, n)] = (t[:, i, :], n - n0)

        def cur_cols(a, n0, n1):
            part, start = cur_tiles[(a, n0)]
            return part[:, start : start + n1 - n0]

        load_p((0, 1))
        nc.scalar.dma_start(out=bounds[8:10, :], in_=avail_bundle.rearrange("(g k) -> g k", g=G))
        nc.scalar.dma_start(out=bounds[10:12, :], in_=alloc_bundle.rearrange("(g k) -> g k", g=G))
        wsc_i = wsc[:].bitcast(I32)
        w_tiles = []

        def load_words(c):
            w = keep.tile([P, G, SC], U8, name="w%d" % c, align_bytes=256)
            nc.sync.dma_start(
                out=w[:].bitcast(I32), in_=words_v[:, :, 1024 * c : 1024 * (c + 1)]
            )
            w_tiles.append(w)

        load_words(0)
        for r in range(4):
            nc.sync.dma_start(out=wsc_i[r:P:32, :, :], in_=scales_v[r])
        load_cur((0,), 0, 2048)
        load_p((2, 3))
        load_words(1)
        load_cur((0,), 2048, 4096)
        load_cur((1,))
        load_cur((2, 3))
        load_p((4, 5, 6, 7))
        load_cur((4, 5, 6, 7))

        hi = keep.tile([P, G * 4], F32, name="hi")
        lo = keep.tile([P, G * 4], F32, name="lo")

        codes = keep.tile([P, NT, G, P], U32, name="codes", align_bytes=256)
        hsc = keep.tile([P, NT, G, P], U8, name="hsc", align_bytes=256)

        tps = {}
        sorted_p = {}

        def sort_columns(a):
            ps = sorted_pool.tile([P, G, 4, P], BF16, name="ps", align_bytes=256)
            columns = p_tiles[a].rearrange("s (g p t) -> s g t p", g=G, p=P, t=4)
            if a == 2:
                nc.gpsimd.tensor_scalar(
                    out=ps[:], in0=columns, scalar1=1.0, scalar2=0.0, op0=ALU.mult, op1=ALU.add
                )
            else:
                nc.scalar.copy(out=ps[:], in_=columns)
            sorted_p[a] = ps

        def transposes(a):
            tp = tpool.tile([P, G * 4, P], BF16, name="tp")
            for g in range(G):
                for t in range(4):
                    if a in sorted_p:
                        columns = sorted_p[a][:, g, t, :]
                    else:
                        columns = p_tiles[a][:, 512 * g + t : 512 * (g + 1) : 4]
                    nc.tensor.transpose(tp[:, 4 * g + t, :], columns, ident[:])
            tps[a] = tp

        def prep_steps(a):
            tp = tps[a]
            r = work.tile([P, G * 4, P], BF16, name="r", align_bytes=256)
            m = work.tile([P, G * 4, P], BF16, name="m", align_bytes=256)
            hg = work.tile([P, G, P, 4], BF16, name="hg", align_bytes=256)

            def clamp(q0, q1):
                for q in range(q0, q1):
                    nc.vector.tensor_scalar(
                        out=r[:, q, :], in0=tp[:, q, :],
                        scalar1=lo[:, q : q + 1], scalar2=hi[:, q : q + 1],
                        op0=ALU.max, op1=ALU.min,
                    )

            def inside():
                nc.vector.tensor_tensor(out=m[:], in0=r[:], in1=tp[:], op=ALU.is_equal)

            def damp(g):
                nc.vector.scalar_tensor_tensor(
                    out=hg[:, g, :, :],
                    in0=m[:, 4 * g : 4 * g + 4, :].rearrange("p t s -> p s t"),
                    scalar=0.01,
                    in1=tp[:, 4 * g : 4 * g + 4, :].rearrange("p t s -> p s t"),
                    op0=ALU.max, op1=ALU.mult,
                )

            def quantise():
                nc.vector.quantize_mx(
                    out=codes[:, a, :, :].rearrange("p g s -> p (g s)").bitcast(FP8X4),
                    scales=hsc[:, a, :, :].rearrange("p g s -> p (g s)"),
                    in_=hg[:].rearrange("p g s t -> p (g s t)"),
                )

            return [
                lambda: clamp(0, 8),
                inside,
                lambda: (damp(0), damp(1)),
                quantise,
            ]

        def product(a, j):
            acc = apool.tile([P, 512], F32, name="acc")
            w = w_tiles[j // 4]
            jj = j % 4
            for g in range(G):
                nc.tensor.matmul_mx(
                    out=acc[:],
                    lhsT=codes[:, a, g, :].bitcast(FP8X4),
                    lhsT_scale=hsc[:, a, g, :],
                    rhs=w[:, g, 1024 * jj : 1024 * (jj + 1)].bitcast(FP4X4),
                    rhs_scale=wsc[:, g, 512 * j : 512 * (j + 1)],
                    start=(g == 0),
                    stop=(g == G - 1),
                )
            return acc

        transposes(0)
        bt = tpool.tile([P, G * 4, P], BF16, name="tp")
        for t in range(4):
            nc.tensor.transpose(bt[:, t, :], bounds[:, t:512:4], ident[:])
        nc.vector.tensor_scalar(
            out=hi[:].rearrange("p (g t) -> p g t", g=G),
            in0=bt[:, 0:4, 8:10].rearrange("p t g -> p g t"),
            scalar1=0.0, scalar2=None, op0=ALU.max,
        )
        nc.vector.tensor_scalar(
            out=lo[:].rearrange("p (g t) -> p g t", g=G),
            in0=bt[:, 0:4, 10:12].rearrange("p t g -> p g t"),
            scalar1=-1.0, scalar2=0.0, op0=ALU.mult, op1=ALU.min,
        )
        sort_columns(1)
        sort_columns(2)
        for step in prep_steps(0):
            step()
        transposes(1)
        pending = prep_steps(1)
        written = 0

        for a in range(NT):
            if a % 2 == 0:
                two_tiles = stage.tile([P, 2, SC], F32, name="two_tiles", align_bytes=256)
            o = two_tiles[:, a % 2, :]
            last = a == NT - 1
            plan = PLAN_LAST if last else PLAN_BODY
            if a == 0:
                pending[0]()
                pending[1]()
                written = 2
            for pos, (j, engine) in enumerate(plan):
                cols = slice(512 * j, 512 * (j + 1))
                acc = product(a, j)
                if engine == "v":
                    nc.vector.tensor_tensor(
                        out=o[:, cols], in0=acc[:], in1=cur_cols(a, 512 * j, 512 * (j + 1)), op=ALU.add
                    )
                    for step in range(2 if a == 1 and pos == 0 else 1):
                        if written < len(pending):
                            pending[written]()
                            written += 1
                else:
                    nc.scalar.copy(out=o[:, cols], in_=acc[:])
                    if j % 2 == 1:
                        pair = slice(512 * (j - 1), 512 * (j + 1))
                        nc.gpsimd.tensor_tensor(
                            out=o[:, pair], in0=o[:, pair],
                            in1=cur_cols(a, 512 * (j - 1), 512 * (j + 1)), op=ALU.add,
                        )
                if pos == (5 if a == 0 else 3) and a + 2 < NT:
                    transposes(a + 2)
                    pending.extend(prep_steps(a + 2))
                if pos == 5 and a + 3 < NT:
                    sort_columns(a + 3)
                if last and pos == 5:
                    nc.sync.dma_start(out=out_v[:, a // 2, a % 2, 0:2048], in_=o[:, 0:2048])
                if last and pos == 7:
                    nc.sync.dma_start(out=out_v[:, a // 2, a % 2, 2048:4096], in_=o[:, 2048:4096])
            if a == 1:
                nc.sync.dma_start(out=out_v[:, 0, :, :], in_=two_tiles[:])
            elif a != 0 and not last:
                nc.sync.dma_start(out=out_v[:, a // 2, a % 2, :], in_=o)
